import numpy as np
import ml_dtypes

BF16 = ml_dtypes.bfloat16


def bf(x):
    return np.asarray(x, np.float32).astype(BF16)


def f32(x):
    return np.asarray(x, np.float32)


def f64(x):
    return np.asarray(x).astype(np.float64)


def striped(idx):
    return np.tile(idx.reshape(-1, 16).T, (8, 1))


D, S, N, M = 128, 256, 64, 256
EPS = 1e-5
THETA = 10000.0


def rope_tables():
    inv_freq = 1.0 / (THETA ** (np.arange(0, D, 2, dtype=np.float32) / D))
    ang = np.arange(N, dtype=np.float32)[:, None] * inv_freq[None, :]
    cos_t = np.ascontiguousarray(np.repeat(np.cos(ang), 2, axis=1).T)
    sin_t = np.ascontiguousarray(np.repeat(np.sin(ang), 2, axis=1).T)
    return cos_t, sin_t


def rot(t):
    r = np.empty_like(t)
    r[0::2] = -t[1::2]
    r[1::2] = t[0::2]
    return r


def setup_inputs():
    cos_t, sin_t = rope_tables()
    scale = np.random.uniform(0.5, 2.0, (1, S))
    shift = 0.5 * np.random.standard_normal((1, S))
    return {"x": bf(scale * np.random.standard_normal((D, S)) + shift), "w": bf(0.5 * np.random.standard_normal((D, M)) / np.sqrt(D)), "gain": f32(1.0 + 0.1 * np.random.standard_normal((D, 1))), "bias": f32(0.1 * np.random.standard_normal((D, 1))), "cos_t": f32(cos_t), "sin_t": f32(sin_t), "offs": striped(np.random.permutation(S)[:N])}


def reference(x, w, gain, bias, cos_t, sin_t, offs):
    idx = offs[:16].T.reshape(-1)
    xs = f64(x)
    mu = xs.mean(axis=0, keepdims=True)
    var = ((xs - mu) ** 2).mean(axis=0, keepdims=True)
    h = (xs - mu) / np.sqrt(var + EPS) * f64(gain) + f64(bias)
    t = f64(w).T @ h[:, idx]
    c = np.tile(f64(cos_t), (M // D, 1))
    s = np.tile(f64(sin_t), (M // D, 1))
    return t * c + rot(t) * s

@@ -1,0 +1,85 @@
+import concourse.mybir as mybir
+
+BF16, F32, U16 = mybir.dt.bfloat16, mybir.dt.float32, mybir.dt.uint16
+ACT = mybir.ActivationFunctionType
+ALU = mybir.AluOpType
+
+D = 128
+S = 256
+N = 64
+M = 256
+HALVES = M // D
+EPS = 1e-5
+
+FLOPS = 2 * D * M * N
+
+
+def tile_blockwiseparallel_kernel(tc, x, w, gain, bias, cos_t, sin_t, offs, out):
+    nc = tc.nc
+    with tc.tile_pool(name="held", bufs=1) as held, tc.psum_pool(name="psum", bufs=1) as psum:
+        x_sb = held.tile([D, S], BF16, name="x_sb")
+        nc.sync.dma_start(x_sb[:], x)
+        offsets = held.tile([D, N // 16], U16, name="offsets")
+        nc.sync.dma_start(offsets[:], offs)
+        w_sb = held.tile([D, M], BF16, name="w_sb")
+        nc.scalar.dma_start(w_sb[:], w)
+        gain_sb = held.tile([D, 1], F32, name="gain_sb")
+        nc.scalar.dma_start(gain_sb[:], gain)
+        bias_sb = held.tile([D, 1], F32, name="bias_sb")
+        nc.scalar.dma_start(bias_sb[:], bias)
+        cos_sin = held.tile([D, 2, N], F32, name="cos_sin")
+        nc.sync.dma_start(cos_sin[:, 0, :], cos_t)
+        nc.sync.dma_start(cos_sin[:, 1, :], sin_t)
+
+        center = held.tile([D, D], BF16, name="center")
+        nc.gpsimd.memset(center[:], -1.0 / D)
+        nc.gpsimd.affine_select(
+            out=center[:],
+            in_=center[:],
+            pattern=[[-1, D]],
+            compare_op=ALU.not_equal,
+            fill=1.0 - 1.0 / D,
+            base=0,
+            channel_multiplier=1,
+        )
+        average = held.tile([D, D], F32, name="average")
+        nc.vector.memset(average[:], 1.0 / D)
+        eps_col = held.tile([D, 1], F32, name="eps_col")
+        nc.vector.memset(eps_col[:], EPS)
+
+        w_rot = held.tile([D, M], BF16, name="w_rot")
+        w_pairs = w_sb[:].rearrange("d (i two) -> d i two", two=2)
+        w_rot_pairs = w_rot[:].rearrange("d (i two) -> d i two", two=2)
+        nc.gpsimd.tensor_scalar_mul(w_rot_pairs[:, :, 0], w_pairs[:, :, 1], -1.0)
+        nc.gpsimd.tensor_copy(w_rot_pairs[:, :, 1], w_pairs[:, :, 0])
+
+        centered = psum.tile([D, S], F32, name="centered")
+        nc.tensor.matmul(centered[:], center[:], x_sb[:], start=True, stop=True)
+        squares = held.tile([D, S], F32, name="squares")
+        nc.scalar.activation(squares[:], centered[:], ACT.Square)
+        variance = psum.tile([D, S], F32, name="variance")
+        nc.tensor.matmul(variance[:], average[:], squares[:], start=True, stop=True)
+        rstd = held.tile([D, S], F32, name="rstd")
+        nc.scalar.activation(rstd[:], variance[:], ACT.Abs_reciprocal_sqrt, bias=eps_col[:], scale=1.0)
+        normed = held.tile([D, S], F32, name="normed")
+        nc.vector.tensor_tensor(normed[:], centered[:], rstd[:], ALU.mult)
+        h = held.tile([D, S], BF16, name="h")
+        nc.vector.tensor_scalar(h[:], normed[:], gain_sb[:], bias_sb[:], ALU.mult, ALU.add)
+
+        projected = psum.tile([D, 2, HALVES, N], F32, name="projected")
+        for k, weights in enumerate((w_sb, w_rot)):
+            for half in range(HALVES):
+                nc.tensor.matmul(
+                    projected[:, k, half, :],
+                    weights[:, half * D : (half + 1) * D],
+                    h[:].indirect(offsets[:]),
+                    start=True,
+                    stop=True,
+                )
+
+        products = held.tile([D, 2, HALVES, N], F32, name="products")
+        tables = cos_sin[:].unsqueeze(2).to_broadcast([D, 2, HALVES, N])
+        nc.vector.tensor_tensor(products[:], projected[:], tables, ALU.mult)
+        out_sb = held.tile([D, HALVES, N], F32, name="out_sb")
+        nc.vector.tensor_tensor(out_sb[:], products[:, 0], products[:, 1], ALU.add)
+        nc.sync.dma_start(out.rearrange("(half d) j -> d half j", half=HALVES), out_sb[:])

@@ -46,6 +46,8 @@ def tile_blockwiseparallel_kernel(tc, x, w, gain, bias, cos_t, sin_t, offs, out)
         nc.vector.memset(average[:], 1.0 / D)
         eps_col = held.tile([D, 1], F32, name="eps_col")
         nc.vector.memset(eps_col[:], EPS)
+        table_warmer = held.tile([D, 1], F32, name="table_warmer")
+        nc.scalar.activation(table_warmer[:], eps_col[:], ACT.Abs_reciprocal_sqrt)
 
         w_rot = held.tile([D, M], BF16, name="w_rot")
         w_pairs = w_sb[:].rearrange("d (i two) -> d i two", two=2)

@@ -9,6 +9,7 @@ S = 256
 N = 64
 M = 256
 HALVES = M // D
+BLOCK = 128
 EPS = 1e-5
 
 FLOPS = 2 * D * M * N
@@ -16,7 +17,13 @@ FLOPS = 2 * D * M * N
 
 def tile_blockwiseparallel_kernel(tc, x, w, gain, bias, cos_t, sin_t, offs, out):
     nc = tc.nc
-    with tc.tile_pool(name="held", bufs=1) as held, tc.psum_pool(name="psum", bufs=1) as psum:
+    with (
+        tc.tile_pool(name="held", bufs=1) as held,
+        tc.tile_pool(name="rope", bufs=HALVES) as rope,
+        tc.tile_pool(name="norm", bufs=S // BLOCK) as norm,
+        tc.psum_pool(name="norm_psum", bufs=S // BLOCK) as norm_psum,
+        tc.psum_pool(name="rope_psum", bufs=HALVES) as rope_psum,
+    ):
         x_sb = held.tile([D, S], BF16, name="x_sb")
         nc.sync.dma_start(x_sb[:], x)
         offsets = held.tile([D, N // 16], U16, name="offsets")
@@ -55,33 +62,35 @@ def tile_blockwiseparallel_kernel(tc, x, w, gain, bias, cos_t, sin_t, offs, out)
         nc.gpsimd.tensor_scalar_mul(w_rot_pairs[:, :, 0], w_pairs[:, :, 1], -1.0)
         nc.gpsimd.tensor_copy(w_rot_pairs[:, :, 1], w_pairs[:, :, 0])
 
-        centered = psum.tile([D, S], F32, name="centered")
-        nc.tensor.matmul(centered[:], center[:], x_sb[:], start=True, stop=True)
-        squares = held.tile([D, S], F32, name="squares")
-        nc.scalar.activation(squares[:], centered[:], ACT.Square)
-        variance = psum.tile([D, S], F32, name="variance")
-        nc.tensor.matmul(variance[:], average[:], squares[:], start=True, stop=True)
-        rstd = held.tile([D, S], F32, name="rstd")
-        nc.scalar.activation(rstd[:], variance[:], ACT.Abs_reciprocal_sqrt, bias=eps_col[:], scale=1.0)
-        normed = held.tile([D, S], F32, name="normed")
-        nc.vector.tensor_tensor(normed[:], centered[:], rstd[:], ALU.mult)
+        blocks = [slice(b * BLOCK, (b + 1) * BLOCK) for b in range(S // BLOCK)]
         h = held.tile([D, S], BF16, name="h")
-        nc.vector.tensor_scalar(h[:], normed[:], gain_sb[:], bias_sb[:], ALU.mult, ALU.add)
+        centered, squares, variance, rstd, normed = [], [], [], [], []
+        for b, cols in enumerate(blocks):
+            centered.append(norm_psum.tile([D, BLOCK], F32, name="centered"))
+            nc.tensor.matmul(centered[b][:], center[:], x_sb[:, cols], start=True, stop=True)
+        for b, cols in enumerate(blocks):
+            squares.append(norm.tile([D, BLOCK], F32, name="squares"))
+            nc.scalar.activation(squares[b][:], centered[b][:], ACT.Square)
+        for b, cols in enumerate(blocks):
+            variance.append(norm_psum.tile([D, BLOCK], F32, name="variance"))
+            nc.tensor.matmul(variance[b][:], average[:], squares[b][:], start=True, stop=True)
+        for b, cols in enumerate(blocks):
+            rstd.append(norm.tile([D, BLOCK], F32, name="rstd"))
+            nc.scalar.activation(rstd[b][:], variance[b][:], ACT.Abs_reciprocal_sqrt, bias=eps_col[:], scale=1.0)
+        for b, cols in enumerate(blocks):
+            normed.append(norm.tile([D, BLOCK], F32, name="normed"))
+            nc.vector.tensor_tensor(normed[b][:], centered[b][:], rstd[b][:], ALU.mult)
+            nc.vector.tensor_scalar(h[:, cols], normed[b][:], gain_sb[:], bias_sb[:], ALU.mult, ALU.add)
 
-        projected = psum.tile([D, 2, HALVES, N], F32, name="projected")
-        for k, weights in enumerate((w_sb, w_rot)):
-            for half in range(HALVES):
+        for half, store_queue in enumerate((nc.scalar, nc.sync)):
+            rows = slice(half * D, (half + 1) * D)
+            projected = rope_psum.tile([D, 2, N], F32, name="projected")
+            for k, weights in enumerate((w_sb, w_rot)):
                 nc.tensor.matmul(
-                    projected[:, k, half, :],
-                    weights[:, half * D : (half + 1) * D],
-                    h[:].indirect(offsets[:]),
-                    start=True,
-                    stop=True,
+                    projected[:, k, :], weights[:, rows], h[:].indirect(offsets[:]), start=True, stop=True
                 )
-
-        products = held.tile([D, 2, HALVES, N], F32, name="products")
-        tables = cos_sin[:].unsqueeze(2).to_broadcast([D, 2, HALVES, N])
-        nc.vector.tensor_tensor(products[:], projected[:], tables, ALU.mult)
-        out_sb = held.tile([D, HALVES, N], F32, name="out_sb")
-        nc.vector.tensor_tensor(out_sb[:], products[:, 0], products[:, 1], ALU.add)
-        nc.sync.dma_start(out.rearrange("(half d) j -> d half j", half=HALVES), out_sb[:])
+            products = rope.tile([D, 2, N], F32, name="products")
+            nc.vector.tensor_tensor(products[:], projected[:], cos_sin[:], ALU.mult)
+            out_sb = rope.tile([D, N], F32, name="out_sb")
+            nc.vector.tensor_tensor(out_sb[:], products[:, 0, :], products[:, 1, :], ALU.add)
+            store_queue.dma_start(out[rows, :], out_sb[:])

@@ -10,6 +10,7 @@ N = 64
 M = 256
 HALVES = M // D
 BLOCK = 128
+WARM_COLUMNS = 512
 EPS = 1e-5
 
 FLOPS = 2 * D * M * N
@@ -23,6 +24,7 @@ def tile_blockwiseparallel_kernel(tc, x, w, gain, bias, cos_t, sin_t, offs, out)
         tc.tile_pool(name="norm", bufs=S // BLOCK) as norm,
         tc.psum_pool(name="norm_psum", bufs=S // BLOCK) as norm_psum,
         tc.psum_pool(name="rope_psum", bufs=HALVES) as rope_psum,
+        tc.psum_pool(name="warm_psum", bufs=1) as warm_psum,
     ):
         x_sb = held.tile([D, S], BF16, name="x_sb")
         nc.sync.dma_start(x_sb[:], x)
@@ -38,6 +40,8 @@ def tile_blockwiseparallel_kernel(tc, x, w, gain, bias, cos_t, sin_t, offs, out)
         nc.sync.dma_start(cos_sin[:, 0, :], cos_t)
         nc.sync.dma_start(cos_sin[:, 1, :], sin_t)
 
+        zeros = held.tile([D, WARM_COLUMNS], BF16, name="zeros")
+        nc.gpsimd.memset(zeros[:], 0.0)
         center = held.tile([D, D], BF16, name="center")
         nc.gpsimd.memset(center[:], -1.0 / D)
         nc.gpsimd.affine_select(
@@ -55,6 +59,14 @@ def tile_blockwiseparallel_kernel(tc, x, w, gain, bias, cos_t, sin_t, offs, out)
         nc.vector.memset(eps_col[:], EPS)
         table_warmer = held.tile([D, 1], F32, name="table_warmer")
         nc.scalar.activation(table_warmer[:], eps_col[:], ACT.Abs_reciprocal_sqrt)
+
+        unread = warm_psum.tile([D, WARM_COLUMNS], F32, name="unread")
+
+        def keep_tensor_engine_busy(matmuls):
+            for m in range(matmuls):
+                nc.tensor.matmul(unread[:], zeros[:, :D], zeros[:], start=True, stop=True)
+
+        keep_tensor_engine_busy(3)
 
         w_rot = held.tile([D, M], BF16, name="w_rot")
         w_pairs = w_sb[:].rearrange("d (i two) -> d i two", two=2)

@@ -10,7 +10,7 @@ N = 64
 M = 256
 HALVES = M // D
 BLOCK = 128
-WARM_COLUMNS = 512
+WARM_COLUMNS = 128
 EPS = 1e-5
 
 FLOPS = 2 * D * M * N
@@ -66,7 +66,7 @@ def tile_blockwiseparallel_kernel(tc, x, w, gain, bias, cos_t, sin_t, offs, out)
             for m in range(matmuls):
                 nc.tensor.matmul(unread[:], zeros[:, :D], zeros[:], start=True, stop=True)
 
-        keep_tensor_engine_busy(3)
+        keep_tensor_engine_busy(12)
 
         w_rot = held.tile([D, M], BF16, name="w_rot")
         w_pairs = w_sb[:].rearrange("d (i two) -> d i two", two=2)

@@ -41,9 +41,9 @@ def tile_blockwiseparallel_kernel(tc, x, w, gain, bias, cos_t, sin_t, offs, out)
         nc.sync.dma_start(cos_sin[:, 1, :], sin_t)
 
         zeros = held.tile([D, WARM_COLUMNS], BF16, name="zeros")
-        nc.gpsimd.memset(zeros[:], 0.0)
+        nc.vector.memset(zeros[:], 0.0)
         center = held.tile([D, D], BF16, name="center")
-        nc.gpsimd.memset(center[:], -1.0 / D)
+        nc.vector.memset(center[:], -1.0 / D)
         nc.gpsimd.affine_select(
             out=center[:],
             in_=center[:],
@@ -66,7 +66,7 @@ def tile_blockwiseparallel_kernel(tc, x, w, gain, bias, cos_t, sin_t, offs, out)
             for m in range(matmuls):
                 nc.tensor.matmul(unread[:], zeros[:, :D], zeros[:], start=True, stop=True)
 
-        keep_tensor_engine_busy(12)
+        keep_tensor_engine_busy(11)
 
         w_rot = held.tile([D, M], BF16, name="w_rot")
         w_pairs = w_sb[:].rearrange("d (i two) -> d i two", two=2)

@@ -33,9 +33,9 @@ def tile_blockwiseparallel_kernel(tc, x, w, gain, bias, cos_t, sin_t, offs, out)
         w_sb = held.tile([D, M], BF16, name="w_sb")
         nc.scalar.dma_start(w_sb[:], w)
         gain_sb = held.tile([D, 1], F32, name="gain_sb")
-        nc.scalar.dma_start(gain_sb[:], gain)
+        nc.sync.dma_start(gain_sb[:], gain)
         bias_sb = held.tile([D, 1], F32, name="bias_sb")
-        nc.scalar.dma_start(bias_sb[:], bias)
+        nc.sync.dma_start(bias_sb[:], bias)
         cos_sin = held.tile([D, 2, N], F32, name="cos_sin")
         nc.sync.dma_start(cos_sin[:, 0, :], cos_t)
         nc.sync.dma_start(cos_sin[:, 1, :], sin_t)

@@ -94,7 +94,7 @@ def tile_blockwiseparallel_kernel(tc, x, w, gain, bias, cos_t, sin_t, offs, out)
             nc.vector.tensor_tensor(normed[b][:], centered[b][:], rstd[b][:], ALU.mult)
             nc.vector.tensor_scalar(h[:, cols], normed[b][:], gain_sb[:], bias_sb[:], ALU.mult, ALU.add)
 
-        for half, store_queue in enumerate((nc.scalar, nc.sync)):
+        for half in range(HALVES):
             rows = slice(half * D, (half + 1) * D)
             projected = rope_psum.tile([D, 2, N], F32, name="projected")
             for k, weights in enumerate((w_sb, w_rot)):
@@ -105,4 +105,4 @@ def tile_blockwiseparallel_kernel(tc, x, w, gain, bias, cos_t, sin_t, offs, out)
             nc.vector.tensor_tensor(products[:], projected[:], cos_sin[:], ALU.mult)
             out_sb = rope.tile([D, N], F32, name="out_sb")
             nc.vector.tensor_tensor(out_sb[:], products[:, 0, :], products[:, 1, :], ALU.add)
-            store_queue.dma_start(out[rows, :], out_sb[:])
+            nc.sync.dma_start(out[rows, :], out_sb[:])

@@ -1,3 +1,5 @@
+import math
+
 import concourse.mybir as mybir
 
 BF16, F32, U16 = mybir.dt.bfloat16, mybir.dt.float32, mybir.dt.uint16
@@ -10,8 +12,10 @@ N = 64
 M = 256
 HALVES = M // D
 BLOCK = 128
+BLOCKS = S // BLOCK
 WARM_COLUMNS = 128
 EPS = 1e-5
+HUGE = 1e29
 
 FLOPS = 2 * D * M * N
 
@@ -21,10 +25,8 @@ def tile_blockwiseparallel_kernel(tc, x, w, gain, bias, cos_t, sin_t, offs, out)
     with (
         tc.tile_pool(name="held", bufs=1) as held,
         tc.tile_pool(name="rope", bufs=HALVES) as rope,
-        tc.tile_pool(name="norm", bufs=S // BLOCK) as norm,
-        tc.psum_pool(name="norm_psum", bufs=S // BLOCK) as norm_psum,
-        tc.psum_pool(name="rope_psum", bufs=HALVES) as rope_psum,
-        tc.psum_pool(name="warm_psum", bufs=1) as warm_psum,
+        tc.tile_pool(name="norm", bufs=BLOCKS) as norm,
+        tc.psum_pool(name="banks", bufs=8) as banks,
     ):
         x_sb = held.tile([D, S], BF16, name="x_sb")
         nc.sync.dma_start(x_sb[:], x)
@@ -53,20 +55,25 @@ def tile_blockwiseparallel_kernel(tc, x, w, gain, bias, cos_t, sin_t, offs, out)
             base=0,
             channel_multiplier=1,
         )
-        average = held.tile([D, D], F32, name="average")
-        nc.vector.memset(average[:], 1.0 / D)
-        eps_col = held.tile([D, 1], F32, name="eps_col")
-        nc.vector.memset(eps_col[:], EPS)
+        eps_diagonal = held.tile([BLOCK, BLOCK], F32, name="eps_diagonal")
+        nc.vector.memset(eps_diagonal[:], HUGE)
+        nc.gpsimd.affine_select(
+            out=eps_diagonal[:],
+            in_=eps_diagonal[:],
+            pattern=[[-1, BLOCK]],
+            compare_op=ALU.not_equal,
+            fill=EPS,
+            base=0,
+            channel_multiplier=1,
+        )
+        one_col = held.tile([D, 1], F32, name="one_col")
+        nc.vector.memset(one_col[:], 1.0)
         table_warmer = held.tile([D, 1], F32, name="table_warmer")
-        nc.scalar.activation(table_warmer[:], eps_col[:], ACT.Abs_reciprocal_sqrt)
+        nc.scalar.activation(table_warmer[:], one_col[:], ACT.Abs_reciprocal_sqrt)
 
-        unread = warm_psum.tile([D, WARM_COLUMNS], F32, name="unread")
-
-        def keep_tensor_engine_busy(matmuls):
-            for m in range(matmuls):
-                nc.tensor.matmul(unread[:], zeros[:, :D], zeros[:], start=True, stop=True)
-
-        keep_tensor_engine_busy(11)
+        unread = banks.tile([D, WARM_COLUMNS], F32, name="unread", tag="bank")
+        for m in range(11):
+            nc.tensor.matmul(unread[:], zeros[:, :D], zeros[:], start=True, stop=True)
 
         w_rot = held.tile([D, M], BF16, name="w_rot")
         w_pairs = w_sb[:].rearrange("d (i two) -> d i two", two=2)
@@ -74,35 +81,42 @@ def tile_blockwiseparallel_kernel(tc, x, w, gain, bias, cos_t, sin_t, offs, out)
         nc.gpsimd.tensor_scalar_mul(w_rot_pairs[:, :, 0], w_pairs[:, :, 1], -1.0)
         nc.gpsimd.tensor_copy(w_rot_pairs[:, :, 1], w_pairs[:, :, 0])
 
-        blocks = [slice(b * BLOCK, (b + 1) * BLOCK) for b in range(S // BLOCK)]
+        blocks = [slice(b * BLOCK, (b + 1) * BLOCK) for b in range(BLOCKS)]
         h = held.tile([D, S], BF16, name="h")
-        centered, squares, variance, rstd, normed = [], [], [], [], []
-        for b, cols in enumerate(blocks):
-            centered.append(norm_psum.tile([D, BLOCK], F32, name="centered"))
-            nc.tensor.matmul(centered[b][:], center[:], x_sb[:, cols], start=True, stop=True)
-        for b, cols in enumerate(blocks):
-            squares.append(norm.tile([D, BLOCK], F32, name="squares"))
-            nc.scalar.activation(squares[b][:], centered[b][:], ACT.Square)
-        for b, cols in enumerate(blocks):
-            variance.append(norm_psum.tile([D, BLOCK], F32, name="variance"))
-            nc.tensor.matmul(variance[b][:], average[:], squares[b][:], start=True, stop=True)
-        for b, cols in enumerate(blocks):
-            rstd.append(norm.tile([D, BLOCK], F32, name="rstd"))
-            nc.scalar.activation(rstd[b][:], variance[b][:], ACT.Abs_reciprocal_sqrt, bias=eps_col[:], scale=1.0)
-        for b, cols in enumerate(blocks):
-            normed.append(norm.tile([D, BLOCK], F32, name="normed"))
-            nc.vector.tensor_tensor(normed[b][:], centered[b][:], rstd[b][:], ALU.mult)
-            nc.vector.tensor_scalar(h[:, cols], normed[b][:], gain_sb[:], bias_sb[:], ALU.mult, ALU.add)
+        for_scalar, for_vector, variance, rows, rstd_diagonal, normed = [], [], [], [], [], []
+        for copies, reader in ((for_scalar, "for_scalar"), (for_vector, "for_vector")):
+            for b, tokens in enumerate(blocks):
+                copies.append(banks.tile([BLOCK, D], F32, name=reader, tag="bank"))
+                nc.tensor.matmul(copies[b][:], x_sb[:, tokens], center[:], start=True, stop=True)
+        for b in range(BLOCKS):
+            squares = norm.tile([BLOCK, D], F32, name="squares")
+            variance.append(norm.tile([BLOCK, 1], F32, name="variance"))
+            nc.scalar.activation(
+                squares[:], for_scalar[b][:], ACT.Square, scale=1.0 / math.sqrt(D), accum_out=variance[b][:]
+            )
+        for b in range(BLOCKS):
+            rows.append(norm.tile([BLOCK, D], F32, name="rows"))
+            nc.vector.tensor_copy(rows[b][:], for_vector[b][:])
+        for b in range(BLOCKS):
+            rstd_diagonal.append(norm.tile([BLOCK, BLOCK], F32, name="rstd_diagonal"))
+            nc.scalar.activation(
+                rstd_diagonal[b][:], eps_diagonal[:], ACT.Abs_reciprocal_sqrt, bias=variance[b][:], scale=1.0
+            )
+        for b, tokens in enumerate(blocks):
+            normed.append(banks.tile([D, BLOCK], F32, name="normed", tag="bank"))
+            nc.tensor.matmul(normed[b][:], rows[b][:], rstd_diagonal[b][:], start=True, stop=True)
+        for b, tokens in enumerate(blocks):
+            nc.vector.tensor_scalar(h[:, tokens], normed[b][:], gain_sb[:], bias_sb[:], ALU.mult, ALU.add)
 
         for half in range(HALVES):
-            rows = slice(half * D, (half + 1) * D)
-            projected = rope_psum.tile([D, 2, N], F32, name="projected")
+            out_rows = slice(half * D, (half + 1) * D)
+            projected = banks.tile([D, 2, N], F32, name="projected", tag="bank")
             for k, weights in enumerate((w_sb, w_rot)):
                 nc.tensor.matmul(
-                    projected[:, k, :], weights[:, rows], h[:].indirect(offsets[:]), start=True, stop=True
+                    projected[:, k, :], weights[:, out_rows], h[:].indirect(offsets[:]), start=True, stop=True
                 )
             products = rope.tile([D, 2, N], F32, name="products")
             nc.vector.tensor_tensor(products[:], projected[:], cos_sin[:], ALU.mult)
             out_sb = rope.tile([D, N], F32, name="out_sb")
             nc.vector.tensor_tensor(out_sb[:], products[:, 0, :], products[:, 1, :], ALU.add)
-            nc.sync.dma_start(out[rows, :], out_sb[:])
+            nc.sync.dma_start(out[out_rows, :], out_sb[:])

@@ -72,7 +72,7 @@ def tile_blockwiseparallel_kernel(tc, x, w, gain, bias, cos_t, sin_t, offs, out)
         nc.scalar.activation(table_warmer[:], one_col[:], ACT.Abs_reciprocal_sqrt)
 
         unread = banks.tile([D, WARM_COLUMNS], F32, name="unread", tag="bank")
-        for m in range(11):
+        for m in range(8):
             nc.tensor.matmul(unread[:], zeros[:, :D], zeros[:], start=True, stop=True)
 
         w_rot = held.tile([D, M], BF16, name="w_rot")

@@ -72,8 +72,12 @@ def tile_blockwiseparallel_kernel(tc, x, w, gain, bias, cos_t, sin_t, offs, out)
         nc.scalar.activation(table_warmer[:], one_col[:], ACT.Abs_reciprocal_sqrt)
 
         unread = banks.tile([D, WARM_COLUMNS], F32, name="unread", tag="bank")
-        for m in range(8):
-            nc.tensor.matmul(unread[:], zeros[:, :D], zeros[:], start=True, stop=True)
+
+        def keep_tensor_engine_busy(matmuls, moving):
+            for m in range(matmuls):
+                nc.tensor.matmul(unread[:], zeros[:, :D], moving[:], start=True, stop=True)
+
+        keep_tensor_engine_busy(8, zeros)
 
         w_rot = held.tile([D, M], BF16, name="w_rot")
         w_pairs = w_sb[:].rearrange("d (i two) -> d i two", two=2)
@@ -89,11 +93,13 @@ def tile_blockwiseparallel_kernel(tc, x, w, gain, bias, cos_t, sin_t, offs, out)
                 copies.append(banks.tile([BLOCK, D], F32, name=reader, tag="bank"))
                 nc.tensor.matmul(copies[b][:], x_sb[:, tokens], center[:], start=True, stop=True)
         for b in range(BLOCKS):
-            squares = norm.tile([BLOCK, D], F32, name="squares")
+            squares = norm.tile([BLOCK, D], BF16, name="squares")
             variance.append(norm.tile([BLOCK, 1], F32, name="variance"))
             nc.scalar.activation(
                 squares[:], for_scalar[b][:], ACT.Square, scale=1.0 / math.sqrt(D), accum_out=variance[b][:]
             )
+            if b == 0:
+                keep_tensor_engine_busy(3, squares)
         for b in range(BLOCKS):
             rows.append(norm.tile([BLOCK, D], F32, name="rows"))
             nc.vector.tensor_copy(rows[b][:], for_vector[b][:])

@@ -73,11 +73,11 @@ def tile_blockwiseparallel_kernel(tc, x, w, gain, bias, cos_t, sin_t, offs, out)
 
         unread = banks.tile([D, WARM_COLUMNS], F32, name="unread", tag="bank")
 
-        def keep_tensor_engine_busy(matmuls, moving):
+        def keep_tensor_engine_busy(matmuls, stationary, moving):
             for m in range(matmuls):
-                nc.tensor.matmul(unread[:], zeros[:, :D], moving[:], start=True, stop=True)
+                nc.tensor.matmul(unread[:], stationary, moving, start=True, stop=True)
 
-        keep_tensor_engine_busy(8, zeros)
+        keep_tensor_engine_busy(8, zeros[:, :D], zeros[:])
 
         w_rot = held.tile([D, M], BF16, name="w_rot")
         w_pairs = w_sb[:].rearrange("d (i two) -> d i two", two=2)
@@ -87,22 +87,20 @@ def tile_blockwiseparallel_kernel(tc, x, w, gain, bias, cos_t, sin_t, offs, out)
 
         blocks = [slice(b * BLOCK, (b + 1) * BLOCK) for b in range(BLOCKS)]
         h = held.tile([D, S], BF16, name="h")
-        for_scalar, for_vector, variance, rows, rstd_diagonal, normed = [], [], [], [], [], []
-        for copies, reader in ((for_scalar, "for_scalar"), (for_vector, "for_vector")):
-            for b, tokens in enumerate(blocks):
-                copies.append(banks.tile([BLOCK, D], F32, name=reader, tag="bank"))
-                nc.tensor.matmul(copies[b][:], x_sb[:, tokens], center[:], start=True, stop=True)
+        centered = [banks.tile([BLOCK, D], F32, name="centered", tag="bank") for b in range(BLOCKS)]
+        for b, tokens in enumerate(blocks):
+            nc.tensor.matmul(centered[b][:], x_sb[:, tokens], center[:], start=True, stop=True)
+        keep_tensor_engine_busy(5, x_sb[:, blocks[0]], center[:])
+        rows = [norm.tile([BLOCK, D], F32, name="rows") for b in range(BLOCKS)]
+        rstd_diagonal, normed = [], []
+        variance = [norm.tile([BLOCK, 1], F32, name="variance") for b in range(BLOCKS)]
         for b in range(BLOCKS):
-            squares = norm.tile([BLOCK, D], BF16, name="squares")
-            variance.append(norm.tile([BLOCK, 1], F32, name="variance"))
+            squares = norm.tile([BLOCK, D], F32, name="squares")
             nc.scalar.activation(
-                squares[:], for_scalar[b][:], ACT.Square, scale=1.0 / math.sqrt(D), accum_out=variance[b][:]
+                squares[:], centered[b][:], ACT.Square, scale=1.0 / math.sqrt(D), accum_out=variance[b][:]
             )
-            if b == 0:
-                keep_tensor_engine_busy(3, squares)
         for b in range(BLOCKS):
-            rows.append(norm.tile([BLOCK, D], F32, name="rows"))
-            nc.vector.tensor_copy(rows[b][:], for_vector[b][:])
+            nc.vector.tensor_copy(rows[b][:], centered[b][:])
         for b in range(BLOCKS):
             rstd_diagonal.append(norm.tile([BLOCK, BLOCK], F32, name="rstd_diagonal"))
             nc.scalar.activation(

@@ -39,8 +39,11 @@ def tile_blockwiseparallel_kernel(tc, x, w, gain, bias, cos_t, sin_t, offs, out)
         bias_sb = held.tile([D, 1], F32, name="bias_sb")
         nc.sync.dma_start(bias_sb[:], bias)
         cos_sin = held.tile([D, 2, N], F32, name="cos_sin")
-        nc.sync.dma_start(cos_sin[:, 0, :], cos_t)
-        nc.sync.dma_start(cos_sin[:, 1, :], sin_t)
+        for k, table in enumerate((cos_t, sin_t)):
+            even_rows = table.rearrange("(pair two) n -> pair two n", two=2)[:, 0, :]
+            for half in range(HALVES):
+                pairs = slice(half * D // 2, (half + 1) * D // 2)
+                nc.sync.dma_start(cos_sin[pairs, k, :], even_rows)
 
         zeros = held.tile([D, WARM_COLUMNS], BF16, name="zeros")
         nc.vector.memset(zeros[:], 0.0)
@@ -79,12 +82,6 @@ def tile_blockwiseparallel_kernel(tc, x, w, gain, bias, cos_t, sin_t, offs, out)
 
         keep_tensor_engine_busy(8, zeros[:, :D], zeros[:])
 
-        w_rot = held.tile([D, M], BF16, name="w_rot")
-        w_pairs = w_sb[:].rearrange("d (i two) -> d i two", two=2)
-        w_rot_pairs = w_rot[:].rearrange("d (i two) -> d i two", two=2)
-        nc.gpsimd.tensor_scalar_mul(w_rot_pairs[:, :, 0], w_pairs[:, :, 1], -1.0)
-        nc.gpsimd.tensor_copy(w_rot_pairs[:, :, 1], w_pairs[:, :, 0])
-
         blocks = [slice(b * BLOCK, (b + 1) * BLOCK) for b in range(BLOCKS)]
         h = held.tile([D, S], BF16, name="h")
         centered = [banks.tile([BLOCK, D], F32, name="centered", tag="bank") for b in range(BLOCKS)]
@@ -112,15 +109,18 @@ def tile_blockwiseparallel_kernel(tc, x, w, gain, bias, cos_t, sin_t, offs, out)
         for b, tokens in enumerate(blocks):
             nc.vector.tensor_scalar(h[:, tokens], normed[b][:], gain_sb[:], bias_sb[:], ALU.mult, ALU.add)
 
-        for half in range(HALVES):
-            out_rows = slice(half * D, (half + 1) * D)
-            projected = banks.tile([D, 2, N], F32, name="projected", tag="bank")
-            for k, weights in enumerate((w_sb, w_rot)):
-                nc.tensor.matmul(
-                    projected[:, k, :], weights[:, out_rows], h[:].indirect(offsets[:]), start=True, stop=True
-                )
-            products = rope.tile([D, 2, N], F32, name="products")
-            nc.vector.tensor_tensor(products[:], projected[:], cos_sin[:], ALU.mult)
-            out_sb = rope.tile([D, N], F32, name="out_sb")
-            nc.vector.tensor_tensor(out_sb[:], products[:, 0, :], products[:, 1, :], ALU.add)
-            nc.sync.dma_start(out[out_rows, :], out_sb[:])
+        even, odd = [banks.tile([M // 2, N], F32, name=name, tag="bank") for name in ("even", "odd")]
+        for parity, projected in enumerate((even, odd)):
+            nc.tensor.matmul(projected[:], w_sb[:, parity::2], h[:].indirect(offsets[:]), start=True, stop=True)
+        even_cos_sin = held.tile([M // 2, 2, N], F32, name="even_cos_sin")
+        nc.vector.tensor_tensor(
+            even_cos_sin[:], even[:].unsqueeze(1).to_broadcast([M // 2, 2, N]), cos_sin[:], ALU.mult
+        )
+        odd_sin, odd_cos = [rope.tile([M // 2, N], F32, name=name) for name in ("odd_sin", "odd_cos")]
+        nc.vector.tensor_tensor(odd_sin[:], odd[:], cos_sin[:, 1, :], ALU.mult)
+        nc.vector.tensor_tensor(odd_cos[:], odd[:], cos_sin[:, 0, :], ALU.mult)
+        out_pairs = out.rearrange("(pair two) n -> pair two n", two=2)
+        for parity, (odd_product, op) in enumerate(((odd_sin, ALU.subtract), (odd_cos, ALU.add))):
+            out_sb = rope.tile([M // 2, N], F32, name="out_sb")
+            nc.vector.tensor_tensor(out_sb[:], even_cos_sin[:, parity, :], odd_product[:], op)
+            nc.sync.dma_start(out_pairs[:, parity, :], out_sb[:])

import math

import concourse.mybir as mybir

BF16, F32, U16 = mybir.dt.bfloat16, mybir.dt.float32, mybir.dt.uint16
ACT = mybir.ActivationFunctionType
ALU = mybir.AluOpType

D = 128
S = 256
N = 64
M = 256
HALVES = M // D
BLOCK = 128
BLOCKS = S // BLOCK
WARM_COLUMNS = 128
EPS = 1e-5
HUGE = 1e29

FLOPS = 2 * D * M * N


def tile_blockwiseparallel_kernel(tc, x, w, gain, bias, cos_t, sin_t, offs, out):
    nc = tc.nc
    with (
        tc.tile_pool(name="held", bufs=1) as held,
        tc.tile_pool(name="rope", bufs=HALVES) as rope,
        tc.tile_pool(name="norm", bufs=BLOCKS) as norm,
        tc.psum_pool(name="banks", bufs=8) as banks,
    ):
        x_sb = held.tile([D, S], BF16, name="x_sb")
        nc.sync.dma_start(x_sb[:], x)
        offsets = held.tile([D, N // 16], U16, name="offsets")
        nc.sync.dma_start(offsets[:], offs)
        w_sb = held.tile([D, M], BF16, name="w_sb")
        nc.scalar.dma_start(w_sb[:], w)
        gain_sb = held.tile([D, 1], F32, name="gain_sb")
        nc.sync.dma_start(gain_sb[:], gain)
        bias_sb = held.tile([D, 1], F32, name="bias_sb")
        nc.sync.dma_start(bias_sb[:], bias)
        cos_sin = held.tile([D, 2, N], F32, name="cos_sin")
        for k, table in enumerate((cos_t, sin_t)):
            even_rows = table.rearrange("(pair two) n -> pair two n", two=2)[:, 0, :]
            for half in range(HALVES):
                pairs = slice(half * D // 2, (half + 1) * D // 2)
                nc.sync.dma_start(cos_sin[pairs, k, :], even_rows)

        zeros = held.tile([D, WARM_COLUMNS], BF16, name="zeros")
        nc.vector.memset(zeros[:], 0.0)
        center = held.tile([D, D], BF16, name="center")
        nc.vector.memset(center[:], -1.0 / D)
        nc.gpsimd.affine_select(
            out=center[:],
            in_=center[:],
            pattern=[[-1, D]],
            compare_op=ALU.not_equal,
            fill=1.0 - 1.0 / D,
            base=0,
            channel_multiplier=1,
        )
        eps_diagonal = held.tile([BLOCK, BLOCK], F32, name="eps_diagonal")
        nc.vector.memset(eps_diagonal[:], HUGE)
        nc.gpsimd.affine_select(
            out=eps_diagonal[:],
            in_=eps_diagonal[:],
            pattern=[[-1, BLOCK]],
            compare_op=ALU.not_equal,
            fill=EPS,
            base=0,
            channel_multiplier=1,
        )
        one_col = held.tile([D, 1], F32, name="one_col")
        nc.vector.memset(one_col[:], 1.0)
        table_warmer = held.tile([D, 1], F32, name="table_warmer")
        nc.scalar.activation(table_warmer[:], one_col[:], ACT.Abs_reciprocal_sqrt)

        unread = banks.tile([D, WARM_COLUMNS], F32, name="unread", tag="bank")

        def keep_tensor_engine_busy(matmuls, stationary, moving):
            for m in range(matmuls):
                nc.tensor.matmul(unread[:], stationary, moving, start=True, stop=True)

        keep_tensor_engine_busy(8, zeros[:, :D], zeros[:])

        blocks = [slice(b * BLOCK, (b + 1) * BLOCK) for b in range(BLOCKS)]
        h = held.tile([D, S], BF16, name="h")
        centered = [banks.tile([BLOCK, D], F32, name="centered", tag="bank") for b in range(BLOCKS)]
        for b, tokens in enumerate(blocks):
            nc.tensor.matmul(centered[b][:], x_sb[:, tokens], center[:], start=True, stop=True)
        keep_tensor_engine_busy(5, x_sb[:, blocks[0]], center[:])
        rows = [norm.tile([BLOCK, D], F32, name="rows") for b in range(BLOCKS)]
        rstd_diagonal, normed = [], []
        variance = [norm.tile([BLOCK, 1], F32, name="variance") for b in range(BLOCKS)]
        for b in range(BLOCKS):
            squares = norm.tile([BLOCK, D], F32, name="squares")
            nc.scalar.activation(
                squares[:], centered[b][:], ACT.Square, scale=1.0 / math.sqrt(D), accum_out=variance[b][:]
            )
        for b in range(BLOCKS):
            nc.vector.tensor_copy(rows[b][:], centered[b][:])
        for b in range(BLOCKS):
            rstd_diagonal.append(norm.tile([BLOCK, BLOCK], F32, name="rstd_diagonal"))
            nc.scalar.activation(
                rstd_diagonal[b][:], eps_diagonal[:], ACT.Abs_reciprocal_sqrt, bias=variance[b][:], scale=1.0
            )
        for b, tokens in enumerate(blocks):
            normed.append(banks.tile([D, BLOCK], F32, name="normed", tag="bank"))
            nc.tensor.matmul(normed[b][:], rows[b][:], rstd_diagonal[b][:], start=True, stop=True)
        for b, tokens in enumerate(blocks):
            nc.vector.tensor_scalar(h[:, tokens], normed[b][:], gain_sb[:], bias_sb[:], ALU.mult, ALU.add)

        even, odd = [banks.tile([M // 2, N], F32, name=name, tag="bank") for name in ("even", "odd")]
        for parity, projected in enumerate((even, odd)):
            nc.tensor.matmul(projected[:], w_sb[:, parity::2], h[:].indirect(offsets[:]), start=True, stop=True)
        even_cos_sin = held.tile([M // 2, 2, N], F32, name="even_cos_sin")
        nc.vector.tensor_tensor(
            even_cos_sin[:], even[:].unsqueeze(1).to_broadcast([M // 2, 2, N]), cos_sin[:], ALU.mult
        )
        odd_sin, odd_cos = [rope.tile([M // 2, N], F32, name=name) for name in ("odd_sin", "odd_cos")]
        nc.vector.tensor_tensor(odd_sin[:], odd[:], cos_sin[:, 1, :], ALU.mult)
        nc.vector.tensor_tensor(odd_cos[:], odd[:], cos_sin[:, 0, :], ALU.mult)
        out_pairs = out.rearrange("(pair two) n -> pair two n", two=2)
        for parity, (odd_product, op) in enumerate(((odd_sin, ALU.subtract), (odd_cos, ALU.add))):
            out_sb = rope.tile([M // 2, N], F32, name="out_sb")
            nc.vector.tensor_tensor(out_sb[:], even_cos_sin[:, parity, :], odd_product[:], op)
            nc.sync.dma_start(out_pairs[:, parity, :], out_sb[:])
